import numpy as np
import ml_dtypes


def mxq(x, axis, fmt="e4m3"):
    dtype, down = {"e4m3": (ml_dtypes.float8_e4m3fn, 7), "e5m2": (ml_dtypes.float8_e5m2, 14)}[fmt]
    v = np.moveaxis(np.asarray(x, np.float32).astype(ml_dtypes.bfloat16).astype(np.float64), axis, -1)
    blocks = v.reshape(v.shape[:-1] + (-1, 32))
    amax = np.abs(blocks).max(-1, keepdims=True)
    byte = np.maximum(np.where(amax > 0, np.frexp(amax)[1] - 1 + 127, 0) - down, 1)
    scale = np.exp2(byte - 127.0)
    codes = (blocks / scale).astype(np.float32).astype(dtype).astype(np.float64)
    return np.moveaxis((codes * scale).reshape(v.shape), -1, axis)


WIDE = False


def mx_kscale(k):
    if not WIDE:
        return np.ones(k)
    levels = np.array([10, -10, 5, -5, 0])
    a = np.random.permutation(np.resize(levels, k // 512 * 4)).reshape(k // 512, 4)
    idx = np.arange(k)
    return np.exp2(a[idx // 512, idx % 128 // 32])


BF16 = ml_dtypes.bfloat16


def bf(x):
    return np.asarray(x, np.float32).astype(BF16)


def f64(x):
    return np.asarray(x).astype(np.float64)


B, S, H, NH, HD = 2, 192, 2048, 16, 128
E = NH * HD
HALF = HD // 2


def rope_tables():
    inv_freq = 1.0 / 10000.0 ** (np.arange(0, HD, 2) / HD)
    pos = np.random.randint(0, S) + np.arange(S)
    freqs = np.outer(pos, inv_freq)
    emb = np.concatenate([freqs, freqs], axis=-1)
    return bf(np.cos(emb)), bf(np.sin(emb))


def apply_rotary(x, cos, sin):
    c = cos[None, None, :, :]
    s = sin[None, None, :, :]
    x1, x2 = x[..., :HALF], x[..., HALF:]
    rotated = np.concatenate([-x2, x1], axis=-1)
    return x * c + rotated * s


def setup_inputs():
    s = mx_kscale(H)
    cos, sin = rope_tables()
    return {"hidden_states": bf(np.random.standard_normal((B, S, H)) * s),
            "cos": cos, "sin": sin,
            "w_qkv": bf(np.random.standard_normal((3 * E, H)) / np.sqrt(H) / s[None, :])}


def reference(hidden_states, cos, sin, w_qkv):
    qkv = mxq(f64(hidden_states), 2, "e4m3") @ mxq(f64(w_qkv), 1, "e4m3").T
    qkv = qkv.reshape(B, S, 3, NH, HD).transpose(2, 0, 3, 1, 4)
    q, k, v = qkv[0], qkv[1], qkv[2]
    q = apply_rotary(q, f64(cos), f64(sin))
    k = apply_rotary(k, f64(cos), f64(sin))
    return q, k, v

@@ -1,0 +1,230 @@
+from contextlib import ExitStack
+
+import concourse.mybir as mybir
+from concourse.masks import make_identity
+
+F32 = mybir.dt.float32
+BF16 = mybir.dt.bfloat16
+U32 = mybir.dt.uint32
+U8 = mybir.dt.uint8
+FP8X4 = mybir.dt.float8_e4m3fn_x4
+MULT = mybir.AluOpType.mult
+ADD = mybir.AluOpType.add
+
+P = 128
+BATCH, SEQ, HIDDEN, HEADS, HEAD_DIM = 2, 192, 2048, 16, 128
+HALF = HEAD_DIM // 2
+WIDTH = HEADS * HEAD_DIM
+TOKEN_TILES = BATCH * SEQ // P
+K_PASS = 4 * P
+PASSES = HIDDEN // K_PASS
+ROW_WORDS = HIDDEN // 2
+PASS_WORDS = K_PASS // 2
+PLANES = PASS_WORDS // P
+PSUM_BANKS = 8
+BANK_WORDS = 512
+BANK_BLOCKS = BANK_WORDS // (PLANES * P)
+QUANT_COLS = 2048
+QUANT_WORDS = QUANT_COLS // 4
+CHUNK_BANKS = QUANT_COLS // 2 // BANK_WORDS
+MAX_ROWS = 4
+GROUPS = WIDTH // (MAX_ROWS * P)
+Q, K, V = 0, 1, 2
+
+RAW_BUFS = 4
+GROUPED_BUFS = 6
+MX_BUFS = 3
+OUT_BUFS = 5
+SWAP_BUFS = 2
+FLIP_BANKS = 4
+ACC_BANKS = PSUM_BANKS - FLIP_BANKS
+
+RUNS = 2
+
+FLOPS = 2 * BATCH * SEQ * HIDDEN * 3 * WIDTH
+
+
+def round_list():
+    order = [(Q, 0), (K, 0)]
+    for group in range(1, GROUPS):
+        order.extend([(Q, group), (K, group), (V, group)])
+    order.append((V, 0))
+    halved = (0, 1, len(order) - 1)
+    rounds = []
+    for place, (kind, group) in enumerate(order):
+        row = kind * WIDTH + group * MAX_ROWS * P
+        pieces = (MAX_ROWS // 2, MAX_ROWS // 2) if place in halved else (MAX_ROWS,)
+        for per in pieces:
+            rounds.append((row, per))
+            row += per * P
+    return rounds
+
+
+def share(count, run):
+    return range(count * run // RUNS, count * (run + 1) // RUNS)
+
+
+def chunk_count(per):
+    return per * PASSES * P // QUANT_WORDS
+
+
+def tile_flashattention_pa_kernel(tc, hidden_states, cos, sin, w_qkv, out_0, out_1, out_2):
+    nc = tc.nc
+    outs = (out_0, out_1, out_2)
+    rounds = round_list()
+
+    with ExitStack() as ctx:
+        const = ctx.enter_context(tc.tile_pool(name="const", bufs=1))
+        raw_pool = ctx.enter_context(tc.tile_pool(name="raw", bufs=RAW_BUFS))
+        grouped_pool = ctx.enter_context(tc.tile_pool(name="grouped", bufs=GROUPED_BUFS))
+        mx_pool = ctx.enter_context(tc.tile_pool(name="mx", bufs=MX_BUFS))
+        out_pool = ctx.enter_context(tc.tile_pool(name="out", bufs=OUT_BUFS))
+        swap_pool = ctx.enter_context(tc.tile_pool(name="swap", bufs=SWAP_BUFS))
+        flip_psum = ctx.enter_context(tc.psum_pool(name="flip", bufs=FLIP_BANKS))
+        acc_psum = ctx.enter_context(tc.psum_pool(name="acc", bufs=ACC_BANKS))
+        ctx.enter_context(tc.manual_schedule())
+
+        def load_tokens(m):
+            raw = const.tile([P, HIDDEN], BF16, name="x_raw%d" % m)
+            for b in range(BATCH):
+                every_third = hidden_states[b].rearrange("(s m) k -> m s k", m=TOKEN_TILES)
+                nc.sync.dma_start(out=raw[b:P:BATCH, :], in_=every_third[m])
+            return raw
+
+        def load_table(table, name):
+            staged = const.tile([P, TOKEN_TILES, HEAD_DIM], BF16, name=name)
+            for b in range(BATCH):
+                nc.sync.dma_start(out=staged[b:P:BATCH, :, :], in_=table.rearrange("(s m) d -> s m d", m=TOKEN_TILES))
+            return staged
+
+        w_raws = []
+
+        def load_next_round():
+            if len(w_raws) < len(rounds):
+                row, per = rounds[len(w_raws)]
+                raw = raw_pool.tile([P, per * HIDDEN], BF16, name="w_raw", tag="w_raw")
+                nc.sync.dma_start(out=raw[:], in_=w_qkv[row : row + per * P, :].rearrange("(p j) k -> p (j k)", j=per))
+                w_raws.append(raw)
+
+        def new_operand(pool, name, per):
+            codes = pool.tile([P, per * PASSES * P], U32, name=name + "_codes", tag=name + "_codes", align_bytes=64)
+            scales = pool.tile([P, per * PASSES * P], U8, name=name + "_scales", tag=name + "_scales", align_bytes=64)
+            return codes, scales
+
+        def fill_operand(operand, raw, per, chunks, vector_helps):
+            codes, scales = operand
+            words = raw[:].bitcast(F32)
+            grouped_tiles = []
+            for chunk in chunks:
+                grouped = grouped_pool.tile([P, QUANT_COLS], BF16, name="grouped", tag="grouped", align_bytes=64)
+                grouped_words = grouped[:].bitcast(F32)
+                for part in range(CHUNK_BANKS):
+                    bank = flip_psum.tile([P, BANK_BLOCKS * PLANES, P], F32, name="bank", tag="bank")
+                    for block in range(BANK_BLOCKS):
+                        g, j = divmod((chunk * CHUNK_BANKS + part) * BANK_BLOCKS + block, per)
+                        for u in range(PLANES):
+                            first = j * ROW_WORDS + g * PASS_WORDS + u * P
+                            nc.tensor.transpose(bank[:, block * PLANES + u, :], words[:, first : first + P], ident[:])
+                    copy = nc.vector.tensor_copy if vector_helps and part == CHUNK_BANKS - 1 else nc.scalar.copy
+                    copy(
+                        out=grouped_words[:, part * BANK_WORDS : (part + 1) * BANK_WORDS].rearrange(
+                            "p (a c u) -> p a c u", a=BANK_BLOCKS, u=PLANES
+                        ),
+                        in_=bank[:].rearrange("p (a u) c -> p a c u", u=PLANES),
+                    )
+                grouped_tiles.append(grouped)
+            for chunk, grouped in zip(chunks, grouped_tiles):
+                cols = slice(chunk * QUANT_WORDS, (chunk + 1) * QUANT_WORDS)
+                nc.vector.quantize_mx(out=codes[:, cols].bitcast(FP8X4), scales=scales[:, cols], in_=grouped[:])
+
+        def one_pass(acc, operand, per, m, g):
+            codes, scales = operand
+            x_codes, x_scales = x_mx[m]
+            width = per * P
+            nc.tensor.matmul_mx(
+                out=acc[:, 0:width],
+                lhsT=x_codes[:, g * P : (g + 1) * P].bitcast(FP8X4),
+                lhsT_scale=x_scales[:, g * P : (g + 1) * P],
+                rhs=codes[:, g * width : (g + 1) * width].bitcast(FP8X4),
+                rhs_scale=scales[:, g * width : (g + 1) * width],
+                start=(g == 0),
+                stop=(g == PASSES - 1),
+            )
+
+        def empty_psum(acc, m, per, result, swapped):
+            quarter = HALF // per
+            lower, upper = slice(0, quarter), slice(quarter, 2 * quarter)
+
+            def of_tile(whole):
+                return whole[:].rearrange("p (h m c j) -> p h m c j", h=per, m=TOKEN_TILES, j=per)[:, :, m, :, :]
+
+            def over_heads(table, some):
+                part = table[:, m, :].rearrange("p (c j) -> p c j", j=per)[:, some, :]
+                return part.unsqueeze(1).to_broadcast([P, per, part.shape[1], per])
+
+            x = acc[:, 0 : per * P].rearrange("p (j h c) -> p h c j", j=per, h=per)
+            if swapped is None:
+                nc.scalar.copy(out=of_tile(result), in_=x)
+                return
+            nc.vector.tensor_tensor(out=of_tile(result), in0=x, in1=over_heads(cos_f32, slice(0, 2 * quarter)), op=MULT)
+            for here, there in ((lower, upper), (upper, lower)):
+                nc.vector.tensor_tensor(
+                    out=of_tile(swapped)[:, :, here, :], in0=x[:, :, there, :], in1=over_heads(sin_signed, here), op=MULT
+                )
+
+        def finish(result, swapped, row, per):
+            if swapped is not None:
+                nc.vector.tensor_tensor(out=result[:], in0=result[:], in1=swapped[:], op=ADD)
+            head = (row % WIDTH) // HEAD_DIM
+            for b in range(BATCH):
+                nc.sync.dma_start(
+                    out=outs[row // WIDTH][b, head : head + per, :, :].rearrange("h (s m) d -> s h (m d)", m=TOKEN_TILES),
+                    in_=result[b:P:BATCH, :].rearrange("p (h f) -> p h f", h=per),
+                )
+
+        x_raws = [load_tokens(m) for m in range(TOKEN_TILES)]
+        load_next_round()
+        load_next_round()
+        cos_bf16 = load_table(cos, "cos_bf16")
+        sin_bf16 = load_table(sin, "sin_bf16")
+        while len(w_raws) < RAW_BUFS:
+            load_next_round()
+
+        ident = const.tile([P, P], F32)
+        make_identity(nc, ident[:])
+
+        x_mx = [new_operand(const, "x%d" % m, 1) for m in range(TOKEN_TILES)]
+        for m in range(TOKEN_TILES):
+            fill_operand(x_mx[m], x_raws[m], 1, range(chunk_count(1)), True)
+        operands = [new_operand(mx_pool, "w", rounds[0][1])]
+        fill_operand(operands[0], w_raws[0], rounds[0][1], range(chunk_count(rounds[0][1])), True)
+        load_next_round()
+
+        cos_f32 = const.tile([P, TOKEN_TILES, HEAD_DIM], F32)
+        sin_signed = const.tile([P, TOKEN_TILES, HEAD_DIM], F32)
+        nc.vector.tensor_copy(out=cos_f32[:], in_=cos_bf16[:])
+        nc.vector.tensor_scalar_mul(out=sin_signed[:, :, 0:HALF], in0=sin_bf16[:, :, 0:HALF], scalar1=-1.0)
+        nc.vector.tensor_copy(out=sin_signed[:, :, HALF:HEAD_DIM], in_=sin_bf16[:, :, HALF:HEAD_DIM])
+
+        passes = [(m, g) for m in range(TOKEN_TILES) for g in range(PASSES)]
+        for i, (row, per) in enumerate(rounds):
+            more = i + 1 < len(rounds)
+            if more:
+                operands.append(new_operand(mx_pool, "w", rounds[i + 1][1]))
+            result = out_pool.tile([P, per * TOKEN_TILES * HEAD_DIM], F32, name="result", tag="result")
+            swapped = None
+            if row < V * WIDTH:
+                swapped = swap_pool.tile([P, per * TOKEN_TILES * HEAD_DIM], F32, name="swapped", tag="swapped")
+            for run in range(RUNS):
+                if more:
+                    coming = rounds[i + 1][1]
+                    fill_operand(operands[i + 1], w_raws[i + 1], coming, share(chunk_count(coming), run), False)
+                for index in share(len(passes), run):
+                    m, g = passes[index]
+                    if g == 0:
+                        acc = acc_psum.tile([P, MAX_ROWS * P], F32, name="acc", tag="acc")
+                    one_pass(acc, operands[i], per, m, g)
+                    if g == PASSES - 1:
+                        empty_psum(acc, m, per, result, swapped)
+            load_next_round()
+            finish(result, swapped, row, per)

@@ -29,13 +29,14 @@ QUANT_WORDS = QUANT_COLS // 4
 CHUNK_BANKS = QUANT_COLS // 2 // BANK_WORDS
 MAX_ROWS = 4
 GROUPS = WIDTH // (MAX_ROWS * P)
+TERMS = 2
 Q, K, V = 0, 1, 2
 
 RAW_BUFS = 4
 GROUPED_BUFS = 6
 MX_BUFS = 3
-OUT_BUFS = 5
-SWAP_BUFS = 2
+ROTATED_BUFS = 4
+PLAIN_BUFS = 3
 FLIP_BANKS = 4
 ACC_BANKS = PSUM_BANKS - FLIP_BANKS
 
@@ -78,8 +79,8 @@ def tile_flashattention_pa_kernel(tc, hidden_states, cos, sin, w_qkv, out_0, out
         raw_pool = ctx.enter_context(tc.tile_pool(name="raw", bufs=RAW_BUFS))
         grouped_pool = ctx.enter_context(tc.tile_pool(name="grouped", bufs=GROUPED_BUFS))
         mx_pool = ctx.enter_context(tc.tile_pool(name="mx", bufs=MX_BUFS))
-        out_pool = ctx.enter_context(tc.tile_pool(name="out", bufs=OUT_BUFS))
-        swap_pool = ctx.enter_context(tc.tile_pool(name="swap", bufs=SWAP_BUFS))
+        rotated_pool = ctx.enter_context(tc.tile_pool(name="rotated", bufs=ROTATED_BUFS))
+        plain_pool = ctx.enter_context(tc.tile_pool(name="plain", bufs=PLAIN_BUFS))
         flip_psum = ctx.enter_context(tc.psum_pool(name="flip", bufs=FLIP_BANKS))
         acc_psum = ctx.enter_context(tc.psum_pool(name="acc", bufs=ACC_BANKS))
         ctx.enter_context(tc.manual_schedule())
@@ -151,35 +152,34 @@ def tile_flashattention_pa_kernel(tc, hidden_states, cos, sin, w_qkv, out_0, out
                 stop=(g == PASSES - 1),
             )
 
-        def empty_psum(acc, m, per, result, swapped):
-            quarter = HALF // per
-            lower, upper = slice(0, quarter), slice(quarter, 2 * quarter)
-
-            def of_tile(whole):
-                return whole[:].rearrange("p (h m c j) -> p h m c j", h=per, m=TOKEN_TILES, j=per)[:, :, m, :, :]
-
-            def over_heads(table, some):
-                part = table[:, m, :].rearrange("p (c j) -> p c j", j=per)[:, some, :]
-                return part.unsqueeze(1).to_broadcast([P, per, part.shape[1], per])
-
+        def empty_psum(acc, m, per, result, rotated):
             x = acc[:, 0 : per * P].rearrange("p (j h c) -> p h c j", j=per, h=per)
-            if swapped is None:
-                nc.scalar.copy(out=of_tile(result), in_=x)
+            if not rotated:
+                out = result[:].rearrange("p (h m c j) -> p h m c j", h=per, m=TOKEN_TILES, j=per)[:, :, m, :, :]
+                nc.scalar.copy(out=out, in_=x)
                 return
-            nc.vector.tensor_tensor(out=of_tile(result), in0=x, in1=over_heads(cos_f32, slice(0, 2 * quarter)), op=MULT)
-            for here, there in ((lower, upper), (upper, lower)):
-                nc.vector.tensor_tensor(
-                    out=of_tile(swapped)[:, :, here, :], in0=x[:, :, there, :], in1=over_heads(sin_signed, here), op=MULT
-                )
+            shape = [P, TERMS, per, P // per, per]
+            nc.vector.tensor_tensor(
+                out=result[:].rearrange("p (w h m c j) -> p w h m c j", w=TERMS, h=per, m=TOKEN_TILES, j=per)[:, :, :, m, :, :],
+                in0=x.unsqueeze(1).to_broadcast(shape),
+                in1=tables[:, m, :, :].rearrange("p w (c j) -> p w c j", j=per).unsqueeze(2).to_broadcast(shape),
+                op=MULT,
+            )
 
-        def finish(result, swapped, row, per):
-            if swapped is not None:
-                nc.vector.tensor_tensor(out=result[:], in0=result[:], in1=swapped[:], op=ADD)
+        def finish(result, rotated, row, per):
+            width = per * TOKEN_TILES * HEAD_DIM
+            if rotated:
+                first = result[:, 0:width].rearrange("p (g s r) -> p g s r", s=2, r=HALF)
+                second = result[:, width : TERMS * width].rearrange("p (g s r) -> p g s r", s=2, r=HALF)
+                for here in range(2):
+                    nc.vector.tensor_tensor(
+                        out=first[:, :, here, :], in0=first[:, :, here, :], in1=second[:, :, 1 - here, :], op=ADD
+                    )
             head = (row % WIDTH) // HEAD_DIM
             for b in range(BATCH):
                 nc.sync.dma_start(
                     out=outs[row // WIDTH][b, head : head + per, :, :].rearrange("h (s m) d -> s h (m d)", m=TOKEN_TILES),
-                    in_=result[b:P:BATCH, :].rearrange("p (h f) -> p h f", h=per),
+                    in_=result[b:P:BATCH, 0:width].rearrange("p (h f) -> p h f", h=per),
                 )
 
         x_raws = [load_tokens(m) for m in range(TOKEN_TILES)]
@@ -200,21 +200,21 @@ def tile_flashattention_pa_kernel(tc, hidden_states, cos, sin, w_qkv, out_0, out
         fill_operand(operands[0], w_raws[0], rounds[0][1], range(chunk_count(rounds[0][1])), True)
         load_next_round()
 
-        cos_f32 = const.tile([P, TOKEN_TILES, HEAD_DIM], F32)
-        sin_signed = const.tile([P, TOKEN_TILES, HEAD_DIM], F32)
-        nc.vector.tensor_copy(out=cos_f32[:], in_=cos_bf16[:])
-        nc.vector.tensor_scalar_mul(out=sin_signed[:, :, 0:HALF], in0=sin_bf16[:, :, 0:HALF], scalar1=-1.0)
-        nc.vector.tensor_copy(out=sin_signed[:, :, HALF:HEAD_DIM], in_=sin_bf16[:, :, HALF:HEAD_DIM])
+        tables = const.tile([P, TOKEN_TILES, TERMS, HEAD_DIM], F32)
+        nc.vector.tensor_copy(out=tables[:, :, 0, :], in_=cos_bf16[:])
+        nc.vector.tensor_copy(out=tables[:, :, 1, 0:HALF], in_=sin_bf16[:, :, HALF:HEAD_DIM])
+        nc.vector.tensor_scalar_mul(out=tables[:, :, 1, HALF:HEAD_DIM], in0=sin_bf16[:, :, 0:HALF], scalar1=-1.0)
 
         passes = [(m, g) for m in range(TOKEN_TILES) for g in range(PASSES)]
         for i, (row, per) in enumerate(rounds):
             more = i + 1 < len(rounds)
             if more:
                 operands.append(new_operand(mx_pool, "w", rounds[i + 1][1]))
-            result = out_pool.tile([P, per * TOKEN_TILES * HEAD_DIM], F32, name="result", tag="result")
-            swapped = None
-            if row < V * WIDTH:
-                swapped = swap_pool.tile([P, per * TOKEN_TILES * HEAD_DIM], F32, name="swapped", tag="swapped")
+            rotated = row < V * WIDTH
+            if rotated:
+                result = rotated_pool.tile([P, TERMS * per * TOKEN_TILES * HEAD_DIM], F32, name="both", tag="both")
+            else:
+                result = plain_pool.tile([P, per * TOKEN_TILES * HEAD_DIM], F32, name="plain", tag="plain")
             for run in range(RUNS):
                 if more:
                     coming = rounds[i + 1][1]
@@ -225,6 +225,6 @@ def tile_flashattention_pa_kernel(tc, hidden_states, cos, sin, w_qkv, out_0, out
                         acc = acc_psum.tile([P, MAX_ROWS * P], F32, name="acc", tag="acc")
                     one_pass(acc, operands[i], per, m, g)
                     if g == PASSES - 1:
-                        empty_psum(acc, m, per, result, swapped)
+                        empty_psum(acc, m, per, result, rotated)
             load_next_round()
-            finish(result, swapped, row, per)
+            finish(result, rotated, row, per)

@@ -41,23 +41,20 @@ FLIP_BANKS = 4
 ACC_BANKS = PSUM_BANKS - FLIP_BANKS
 
 RUNS = 2
+UNIT_ROWS = 2
+PLAN = [(Q,0,0,2),(Q,0,2,2),(K,0,0,2),(K,0,2,2),(Q,1,0,4),(K,1,0,4),(V,1,0,4),(Q,2,0,4),(K,2,0,4),(V,2,0,4),(Q,3,0,4),(K,3,0,4),(V,3,0,4),(V,0,0,2),(V,0,2,2),]
+LEAD_EARLY = 2
+EARLY_UNITS = 3
+LEAD = 3
+HELPED_UNITS = 2
 
 FLOPS = 2 * BATCH * SEQ * HIDDEN * 3 * WIDTH
 
 
 def round_list():
-    order = [(Q, 0), (K, 0)]
-    for group in range(1, GROUPS):
-        order.extend([(Q, group), (K, group), (V, group)])
-    order.append((V, 0))
-    halved = (0, 1, len(order) - 1)
     rounds = []
-    for place, (kind, group) in enumerate(order):
-        row = kind * WIDTH + group * MAX_ROWS * P
-        pieces = (MAX_ROWS // 2, MAX_ROWS // 2) if place in halved else (MAX_ROWS,)
-        for per in pieces:
-            rounds.append((row, per))
-            row += per * P
+    for kind, group, first, per in PLAN:
+        rounds.append((kind * WIDTH + group * MAX_ROWS * P + first * P, per))
     return rounds
 
 
@@ -99,6 +96,7 @@ def tile_flashattention_pa_kernel(tc, hidden_states, cos, sin, w_qkv, out_0, out
             return staged
 
         w_raws = []
+        jobs = []
 
         def load_next_round():
             if len(w_raws) < len(rounds):
@@ -137,6 +135,8 @@ def tile_flashattention_pa_kernel(tc, hidden_states, cos, sin, w_qkv, out_0, out
             for chunk, grouped in zip(chunks, grouped_tiles):
                 cols = slice(chunk * QUANT_WORDS, (chunk + 1) * QUANT_WORDS)
                 nc.vector.quantize_mx(out=codes[:, cols].bitcast(FP8X4), scales=scales[:, cols], in_=grouped[:])
+                if jobs:
+                    jobs.pop(0)()
 
         def one_pass(acc, operand, per, m, g):
             codes, scales = operand
@@ -166,21 +166,29 @@ def tile_flashattention_pa_kernel(tc, hidden_states, cos, sin, w_qkv, out_0, out
                 op=MULT,
             )
 
-        def finish(result, rotated, row, per):
+        def add_half(result, per, here):
             width = per * TOKEN_TILES * HEAD_DIM
-            if rotated:
-                first = result[:, 0:width].rearrange("p (g s r) -> p g s r", s=2, r=HALF)
-                second = result[:, width : TERMS * width].rearrange("p (g s r) -> p g s r", s=2, r=HALF)
-                for here in range(2):
-                    nc.vector.tensor_tensor(
-                        out=first[:, :, here, :], in0=first[:, :, here, :], in1=second[:, :, 1 - here, :], op=ADD
-                    )
+            first = result[:, 0:width].rearrange("p (g s r) -> p g s r", s=2, r=HALF)
+            second = result[:, width : TERMS * width].rearrange("p (g s r) -> p g s r", s=2, r=HALF)
+            nc.vector.tensor_tensor(out=first[:, :, here, :], in0=first[:, :, here, :], in1=second[:, :, 1 - here, :], op=ADD)
+
+        def store(result, row, per):
+            width = per * TOKEN_TILES * HEAD_DIM
             head = (row % WIDTH) // HEAD_DIM
             for b in range(BATCH):
                 nc.sync.dma_start(
                     out=outs[row // WIDTH][b, head : head + per, :, :].rearrange("h (s m) d -> s h (m d)", m=TOKEN_TILES),
                     in_=result[b:P:BATCH, 0:width].rearrange("p (h f) -> p h f", h=per),
                 )
+
+        def lower_job(result, per):
+            return lambda: add_half(result, per, 0)
+
+        def upper_job(result, row, per):
+            def job():
+                add_half(result, per, 1)
+                store(result, row, per)
+            return job
 
         x_raws = [load_tokens(m) for m in range(TOKEN_TILES)]
         load_next_round()
@@ -196,35 +204,68 @@ def tile_flashattention_pa_kernel(tc, hidden_states, cos, sin, w_qkv, out_0, out
         x_mx = [new_operand(const, "x%d" % m, 1) for m in range(TOKEN_TILES)]
         for m in range(TOKEN_TILES):
             fill_operand(x_mx[m], x_raws[m], 1, range(chunk_count(1)), True)
-        operands = [new_operand(mx_pool, "w", rounds[0][1])]
-        fill_operand(operands[0], w_raws[0], rounds[0][1], range(chunk_count(rounds[0][1])), True)
-        load_next_round()
 
         tables = const.tile([P, TOKEN_TILES, TERMS, HEAD_DIM], F32)
-        nc.vector.tensor_copy(out=tables[:, :, 0, :], in_=cos_bf16[:])
-        nc.vector.tensor_copy(out=tables[:, :, 1, 0:HALF], in_=sin_bf16[:, :, HALF:HEAD_DIM])
-        nc.vector.tensor_scalar_mul(out=tables[:, :, 1, HALF:HEAD_DIM], in0=sin_bf16[:, :, 0:HALF], scalar1=-1.0)
 
-        passes = [(m, g) for m in range(TOKEN_TILES) for g in range(PASSES)]
+        def make_tables():
+            nc.vector.tensor_copy(out=tables[:, :, 0, :], in_=cos_bf16[:])
+            nc.vector.tensor_copy(out=tables[:, :, 1, 0:HALF], in_=sin_bf16[:, :, HALF:HEAD_DIM])
+            nc.vector.tensor_scalar_mul(out=tables[:, :, 1, HALF:HEAD_DIM], in0=sin_bf16[:, :, 0:HALF], scalar1=-1.0)
+
+        units = []
         for i, (row, per) in enumerate(rounds):
-            more = i + 1 < len(rounds)
-            if more:
-                operands.append(new_operand(mx_pool, "w", rounds[i + 1][1]))
+            for part in range(per // UNIT_ROWS):
+                units.append((i, part, per // UNIT_ROWS))
+        passes = [(m, g) for m in range(TOKEN_TILES) for g in range(PASSES)]
+        operands = {}
+        results = {}
+        accs = {}
+
+        def part_of(count, part, parts):
+            return range(count * part // parts, count * (part + 1) // parts)
+
+        def flip_unit(u):
+            i, part, parts = units[u]
+            per = rounds[i][1]
+            if part == 0:
+                operands[i] = new_operand(mx_pool, "w", per)
+            fill_operand(operands[i], w_raws[i], per, part_of(chunk_count(per), part, parts), u < HELPED_UNITS)
+            if part == parts - 1:
+                load_next_round()
+
+        def multiply_unit(u):
+            i, part, parts = units[u]
+            row, per = rounds[i]
             rotated = row < V * WIDTH
-            if rotated:
-                result = rotated_pool.tile([P, TERMS * per * TOKEN_TILES * HEAD_DIM], F32, name="both", tag="both")
-            else:
-                result = plain_pool.tile([P, per * TOKEN_TILES * HEAD_DIM], F32, name="plain", tag="plain")
-            for run in range(RUNS):
-                if more:
-                    coming = rounds[i + 1][1]
-                    fill_operand(operands[i + 1], w_raws[i + 1], coming, share(chunk_count(coming), run), False)
-                for index in share(len(passes), run):
-                    m, g = passes[index]
-                    if g == 0:
-                        acc = acc_psum.tile([P, MAX_ROWS * P], F32, name="acc", tag="acc")
-                    one_pass(acc, operands[i], per, m, g)
-                    if g == PASSES - 1:
-                        empty_psum(acc, m, per, result, rotated)
-            load_next_round()
-            finish(result, rotated, row, per)
+            if part == 0:
+                if rotated:
+                    results[i] = rotated_pool.tile([P, TERMS * per * TOKEN_TILES * HEAD_DIM], F32, name="both", tag="both")
+                else:
+                    results[i] = plain_pool.tile([P, per * TOKEN_TILES * HEAD_DIM], F32, name="plain", tag="plain")
+            for index in part_of(len(passes), part, parts):
+                m, g = passes[index]
+                if g == 0:
+                    accs[0] = acc_psum.tile([P, MAX_ROWS * P], F32, name="acc", tag="acc")
+                one_pass(accs[0], operands[i], per, m, g)
+                if g == PASSES - 1:
+                    empty_psum(accs[0], m, per, results[i], rotated)
+            if part == parts - 1:
+                if rotated:
+                    jobs.append(lower_job(results[i], per))
+                    jobs.append(upper_job(results[i], row, per))
+                else:
+                    store(results[i], row, per)
+
+        flipped = 0
+        for u in range(len(units)):
+            lead = LEAD_EARLY if u < EARLY_UNITS else LEAD
+            while flipped < min(len(units), u + lead):
+                flip_unit(flipped)
+                flipped += 1
+            if u == 0:
+                make_tables()
+            while jobs:
+                jobs.pop(0)()
+            multiply_unit(u)
+        while jobs:
+            jobs.pop(0)()

@@ -96,7 +96,6 @@ def tile_flashattention_pa_kernel(tc, hidden_states, cos, sin, w_qkv, out_0, out
             return staged
 
         w_raws = []
-        jobs = []
 
         def load_next_round():
             if len(w_raws) < len(rounds):
@@ -135,8 +134,6 @@ def tile_flashattention_pa_kernel(tc, hidden_states, cos, sin, w_qkv, out_0, out
             for chunk, grouped in zip(chunks, grouped_tiles):
                 cols = slice(chunk * QUANT_WORDS, (chunk + 1) * QUANT_WORDS)
                 nc.vector.quantize_mx(out=codes[:, cols].bitcast(FP8X4), scales=scales[:, cols], in_=grouped[:])
-                if jobs:
-                    jobs.pop(0)()
 
         def one_pass(acc, operand, per, m, g):
             codes, scales = operand
@@ -166,11 +163,14 @@ def tile_flashattention_pa_kernel(tc, hidden_states, cos, sin, w_qkv, out_0, out
                 op=MULT,
             )
 
-        def add_half(result, per, here):
+        def add_tile(result, per, m):
             width = per * TOKEN_TILES * HEAD_DIM
-            first = result[:, 0:width].rearrange("p (g s r) -> p g s r", s=2, r=HALF)
-            second = result[:, width : TERMS * width].rearrange("p (g s r) -> p g s r", s=2, r=HALF)
-            nc.vector.tensor_tensor(out=first[:, :, here, :], in0=first[:, :, here, :], in1=second[:, :, 1 - here, :], op=ADD)
+            first = result[:, 0:width].rearrange("p (h m s r) -> p h m s r", h=per, m=TOKEN_TILES, s=2)
+            second = result[:, width : TERMS * width].rearrange("p (h m s r) -> p h m s r", h=per, m=TOKEN_TILES, s=2)
+            for here in range(2):
+                nc.vector.tensor_tensor(
+                    out=first[:, :, m, here, :], in0=first[:, :, m, here, :], in1=second[:, :, m, 1 - here, :], op=ADD
+                )
 
         def store(result, row, per):
             width = per * TOKEN_TILES * HEAD_DIM
@@ -180,15 +180,6 @@ def tile_flashattention_pa_kernel(tc, hidden_states, cos, sin, w_qkv, out_0, out
                     out=outs[row // WIDTH][b, head : head + per, :, :].rearrange("h (s m) d -> s h (m d)", m=TOKEN_TILES),
                     in_=result[b:P:BATCH, 0:width].rearrange("p (h f) -> p h f", h=per),
                 )
-
-        def lower_job(result, per):
-            return lambda: add_half(result, per, 0)
-
-        def upper_job(result, row, per):
-            def job():
-                add_half(result, per, 1)
-                store(result, row, per)
-            return job
 
         x_raws = [load_tokens(m) for m in range(TOKEN_TILES)]
         load_next_round()
@@ -249,12 +240,12 @@ def tile_flashattention_pa_kernel(tc, hidden_states, cos, sin, w_qkv, out_0, out
                 one_pass(accs[0], operands[i], per, m, g)
                 if g == PASSES - 1:
                     empty_psum(accs[0], m, per, results[i], rotated)
+                    if rotated and m > 0:
+                        add_tile(results[i], per, m - 1)
             if part == parts - 1:
                 if rotated:
-                    jobs.append(lower_job(results[i], per))
-                    jobs.append(upper_job(results[i], row, per))
-                else:
-                    store(results[i], row, per)
+                    add_tile(results[i], per, TOKEN_TILES - 1)
+                store(results[i], row, per)
 
         flipped = 0
         for u in range(len(units)):
@@ -264,8 +255,4 @@ def tile_flashattention_pa_kernel(tc, hidden_states, cos, sin, w_qkv, out_0, out
                 flipped += 1
             if u == 0:
                 make_tables()
-            while jobs:
-                jobs.pop(0)()
             multiply_unit(u)
-        while jobs:
-            jobs.pop(0)()

@@ -47,6 +47,8 @@ LEAD_EARLY = 2
 EARLY_UNITS = 3
 LEAD = 3
 HELPED_UNITS = 2
+WARM_UP = 6
+KEEP_WARM = (1, 1, 4, 2)
 
 FLOPS = 2 * BATCH * SEQ * HIDDEN * 3 * WIDTH
 
@@ -192,9 +194,20 @@ def tile_flashattention_pa_kernel(tc, hidden_states, cos, sin, w_qkv, out_0, out
         ident = const.tile([P, P], F32)
         make_identity(nc, ident[:])
 
+        zeros = const.tile([P, BANK_WORDS], BF16)
+        nc.vector.memset(zeros[:], 0.0)
+        unread = acc_psum.tile([P, MAX_ROWS * P], F32, name="acc", tag="acc")
+
+        def idle_matmuls(count):
+            for turn in range(count):
+                nc.tensor.matmul(out=unread[:], lhsT=zeros[:, 0:P], rhs=zeros[:], start=True, stop=True)
+
+        idle_matmuls(WARM_UP)
+
         x_mx = [new_operand(const, "x%d" % m, 1) for m in range(TOKEN_TILES)]
         for m in range(TOKEN_TILES):
             fill_operand(x_mx[m], x_raws[m], 1, range(chunk_count(1)), True)
+            idle_matmuls(KEEP_WARM[m])
 
         tables = const.tile([P, TOKEN_TILES, TERMS, HEAD_DIM], F32)
 
@@ -252,6 +265,8 @@ def tile_flashattention_pa_kernel(tc, hidden_states, cos, sin, w_qkv, out_0, out
             lead = LEAD_EARLY if u < EARLY_UNITS else LEAD
             while flipped < min(len(units), u + lead):
                 flip_unit(flipped)
+                if flipped == 0:
+                    idle_matmuls(KEEP_WARM[TOKEN_TILES])
                 flipped += 1
             if u == 0:
                 make_tables()

@@ -228,6 +228,15 @@ def tile_flashattention_pa_kernel(tc, hidden_states, cos, sin, w_qkv, out_0, out
         def part_of(count, part, parts):
             return range(count * part // parts, count * (part + 1) // parts)
 
+        waiting = []
+
+        def is_rotated(i):
+            return rounds[i][0] < V * WIDTH
+
+        def put_off(i):
+            plain = [j for j in range(i + 1, len(rounds)) if not is_rotated(j)]
+            return is_rotated(i) and rounds[i][1] == MAX_ROWS and any(is_rotated(j) for j in range(plain[0], len(rounds)))
+
         def flip_unit(u):
             i, part, parts = units[u]
             per = rounds[i][1]
@@ -253,12 +262,20 @@ def tile_flashattention_pa_kernel(tc, hidden_states, cos, sin, w_qkv, out_0, out
                 one_pass(accs[0], operands[i], per, m, g)
                 if g == PASSES - 1:
                     empty_psum(accs[0], m, per, results[i], rotated)
-                    if rotated and m > 0:
+                    if rotated and m > 0 and not put_off(i):
                         add_tile(results[i], per, m - 1)
+            if not rotated and waiting:
+                late = waiting.pop(0)
+                for m in range(TOKEN_TILES):
+                    add_tile(results[late], rounds[late][1], m)
+                store(results[late], rounds[late][0], rounds[late][1])
             if part == parts - 1:
-                if rotated:
-                    add_tile(results[i], per, TOKEN_TILES - 1)
-                store(results[i], row, per)
+                if rotated and put_off(i):
+                    waiting.append(i)
+                else:
+                    if rotated:
+                        add_tile(results[i], per, TOKEN_TILES - 1)
+                    store(results[i], row, per)
 
         flipped = 0
         for u in range(len(units)):

@@ -44,7 +44,7 @@ RUNS = 2
 UNIT_ROWS = 2
 PLAN = [(Q,0,0,2),(Q,0,2,2),(K,0,0,2),(K,0,2,2),(Q,1,0,4),(K,1,0,4),(V,1,0,4),(Q,2,0,4),(K,2,0,4),(V,2,0,4),(Q,3,0,4),(K,3,0,4),(V,3,0,4),(V,0,0,2),(V,0,2,2),]
 LEAD_EARLY = 2
-EARLY_UNITS = 3
+EARLY_UNITS = 2
 LEAD = 3
 HELPED_UNITS = 2
 WARM_UP = 6
@@ -246,10 +246,11 @@ def tile_flashattention_pa_kernel(tc, hidden_states, cos, sin, w_qkv, out_0, out
             if part == parts - 1:
                 load_next_round()
 
-        def multiply_unit(u):
+        def multiply_unit(u, piece, pieces):
             i, part, parts = units[u]
             row, per = rounds[i]
             rotated = row < V * WIDTH
+            part, parts = part * pieces + piece, parts * pieces
             if part == 0:
                 if rotated:
                     results[i] = rotated_pool.tile([P, TERMS * per * TOKEN_TILES * HEAD_DIM], F32, name="both", tag="both")
@@ -280,11 +281,14 @@ def tile_flashattention_pa_kernel(tc, hidden_states, cos, sin, w_qkv, out_0, out
         flipped = 0
         for u in range(len(units)):
             lead = LEAD_EARLY if u < EARLY_UNITS else LEAD
-            while flipped < min(len(units), u + lead):
-                flip_unit(flipped)
-                if flipped == 0:
-                    idle_matmuls(KEEP_WARM[TOKEN_TILES])
-                flipped += 1
-            if u == 0:
-                make_tables()
-            multiply_unit(u)
+            due = min(len(units), u + lead) - flipped
+            pieces = due if u > 0 and due > 1 else 1
+            for piece in range(pieces):
+                while flipped < min(len(units), u + lead) - (pieces - 1 - piece):
+                    flip_unit(flipped)
+                    if flipped == 0:
+                        idle_matmuls(KEEP_WARM[TOKEN_TILES])
+                    flipped += 1
+                if u == 0:
+                    make_tables()
+                multiply_unit(u, piece, pieces)

from contextlib import ExitStack

import concourse.mybir as mybir
from concourse.masks import make_identity

F32 = mybir.dt.float32
BF16 = mybir.dt.bfloat16
U32 = mybir.dt.uint32
U8 = mybir.dt.uint8
FP8X4 = mybir.dt.float8_e4m3fn_x4
MULT = mybir.AluOpType.mult
ADD = mybir.AluOpType.add

P = 128
BATCH, SEQ, HIDDEN, HEADS, HEAD_DIM = 2, 192, 2048, 16, 128
HALF = HEAD_DIM // 2
WIDTH = HEADS * HEAD_DIM
TOKEN_TILES = BATCH * SEQ // P
K_PASS = 4 * P
PASSES = HIDDEN // K_PASS
ROW_WORDS = HIDDEN // 2
PASS_WORDS = K_PASS // 2
PLANES = PASS_WORDS // P
PSUM_BANKS = 8
BANK_WORDS = 512
BANK_BLOCKS = BANK_WORDS // (PLANES * P)
QUANT_COLS = 2048
QUANT_WORDS = QUANT_COLS // 4
CHUNK_BANKS = QUANT_COLS // 2 // BANK_WORDS
MAX_ROWS = 4
GROUPS = WIDTH // (MAX_ROWS * P)
TERMS = 2
Q, K, V = 0, 1, 2

RAW_BUFS = 4
GROUPED_BUFS = 6
MX_BUFS = 3
ROTATED_BUFS = 4
PLAIN_BUFS = 3
FLIP_BANKS = 4
ACC_BANKS = PSUM_BANKS - FLIP_BANKS

RUNS = 2
UNIT_ROWS = 2
PLAN = [(Q,0,0,2),(Q,0,2,2),(K,0,0,2),(K,0,2,2),(Q,1,0,4),(K,1,0,4),(V,1,0,4),(Q,2,0,4),(K,2,0,4),(V,2,0,4),(Q,3,0,4),(K,3,0,4),(V,3,0,4),(V,0,0,2),(V,0,2,2),]
LEAD_EARLY = 2
EARLY_UNITS = 2
LEAD = 3
HELPED_UNITS = 2
WARM_UP = 6
KEEP_WARM = (1, 1, 4, 2)

FLOPS = 2 * BATCH * SEQ * HIDDEN * 3 * WIDTH


def round_list():
    rounds = []
    for kind, group, first, per in PLAN:
        rounds.append((kind * WIDTH + group * MAX_ROWS * P + first * P, per))
    return rounds


def share(count, run):
    return range(count * run // RUNS, count * (run + 1) // RUNS)


def chunk_count(per):
    return per * PASSES * P // QUANT_WORDS


def tile_flashattention_pa_kernel(tc, hidden_states, cos, sin, w_qkv, out_0, out_1, out_2):
    nc = tc.nc
    outs = (out_0, out_1, out_2)
    rounds = round_list()

    with ExitStack() as ctx:
        const = ctx.enter_context(tc.tile_pool(name="const", bufs=1))
        raw_pool = ctx.enter_context(tc.tile_pool(name="raw", bufs=RAW_BUFS))
        grouped_pool = ctx.enter_context(tc.tile_pool(name="grouped", bufs=GROUPED_BUFS))
        mx_pool = ctx.enter_context(tc.tile_pool(name="mx", bufs=MX_BUFS))
        rotated_pool = ctx.enter_context(tc.tile_pool(name="rotated", bufs=ROTATED_BUFS))
        plain_pool = ctx.enter_context(tc.tile_pool(name="plain", bufs=PLAIN_BUFS))
        flip_psum = ctx.enter_context(tc.psum_pool(name="flip", bufs=FLIP_BANKS))
        acc_psum = ctx.enter_context(tc.psum_pool(name="acc", bufs=ACC_BANKS))
        ctx.enter_context(tc.manual_schedule())

        def load_tokens(m):
            raw = const.tile([P, HIDDEN], BF16, name="x_raw%d" % m)
            for b in range(BATCH):
                every_third = hidden_states[b].rearrange("(s m) k -> m s k", m=TOKEN_TILES)
                nc.sync.dma_start(out=raw[b:P:BATCH, :], in_=every_third[m])
            return raw

        def load_table(table, name):
            staged = const.tile([P, TOKEN_TILES, HEAD_DIM], BF16, name=name)
            for b in range(BATCH):
                nc.sync.dma_start(out=staged[b:P:BATCH, :, :], in_=table.rearrange("(s m) d -> s m d", m=TOKEN_TILES))
            return staged

        w_raws = []

        def load_next_round():
            if len(w_raws) < len(rounds):
                row, per = rounds[len(w_raws)]
                raw = raw_pool.tile([P, per * HIDDEN], BF16, name="w_raw", tag="w_raw")
                nc.sync.dma_start(out=raw[:], in_=w_qkv[row : row + per * P, :].rearrange("(p j) k -> p (j k)", j=per))
                w_raws.append(raw)

        def new_operand(pool, name, per):
            codes = pool.tile([P, per * PASSES * P], U32, name=name + "_codes", tag=name + "_codes", align_bytes=64)
            scales = pool.tile([P, per * PASSES * P], U8, name=name + "_scales", tag=name + "_scales", align_bytes=64)
            return codes, scales

        def fill_operand(operand, raw, per, chunks, vector_helps):
            codes, scales = operand
            words = raw[:].bitcast(F32)
            grouped_tiles = []
            for chunk in chunks:
                grouped = grouped_pool.tile([P, QUANT_COLS], BF16, name="grouped", tag="grouped", align_bytes=64)
                grouped_words = grouped[:].bitcast(F32)
                for part in range(CHUNK_BANKS):
                    bank = flip_psum.tile([P, BANK_BLOCKS * PLANES, P], F32, name="bank", tag="bank")
                    for block in range(BANK_BLOCKS):
                        g, j = divmod((chunk * CHUNK_BANKS + part) * BANK_BLOCKS + block, per)
                        for u in range(PLANES):
                            first = j * ROW_WORDS + g * PASS_WORDS + u * P
                            nc.tensor.transpose(bank[:, block * PLANES + u, :], words[:, first : first + P], ident[:])
                    copy = nc.vector.tensor_copy if vector_helps and part == CHUNK_BANKS - 1 else nc.scalar.copy
                    copy(
                        out=grouped_words[:, part * BANK_WORDS : (part + 1) * BANK_WORDS].rearrange(
                            "p (a c u) -> p a c u", a=BANK_BLOCKS, u=PLANES
                        ),
                        in_=bank[:].rearrange("p (a u) c -> p a c u", u=PLANES),
                    )
                grouped_tiles.append(grouped)
            for chunk, grouped in zip(chunks, grouped_tiles):
                cols = slice(chunk * QUANT_WORDS, (chunk + 1) * QUANT_WORDS)
                nc.vector.quantize_mx(out=codes[:, cols].bitcast(FP8X4), scales=scales[:, cols], in_=grouped[:])

        def one_pass(acc, operand, per, m, g):
            codes, scales = operand
            x_codes, x_scales = x_mx[m]
            width = per * P
            nc.tensor.matmul_mx(
                out=acc[:, 0:width],
                lhsT=x_codes[:, g * P : (g + 1) * P].bitcast(FP8X4),
                lhsT_scale=x_scales[:, g * P : (g + 1) * P],
                rhs=codes[:, g * width : (g + 1) * width].bitcast(FP8X4),
                rhs_scale=scales[:, g * width : (g + 1) * width],
                start=(g == 0),
                stop=(g == PASSES - 1),
            )

        def empty_psum(acc, m, per, result, rotated):
            x = acc[:, 0 : per * P].rearrange("p (j h c) -> p h c j", j=per, h=per)
            if not rotated:
                out = result[:].rearrange("p (h m c j) -> p h m c j", h=per, m=TOKEN_TILES, j=per)[:, :, m, :, :]
                nc.scalar.copy(out=out, in_=x)
                return
            shape = [P, TERMS, per, P // per, per]
            nc.vector.tensor_tensor(
                out=result[:].rearrange("p (w h m c j) -> p w h m c j", w=TERMS, h=per, m=TOKEN_TILES, j=per)[:, :, :, m, :, :],
                in0=x.unsqueeze(1).to_broadcast(shape),
                in1=tables[:, m, :, :].rearrange("p w (c j) -> p w c j", j=per).unsqueeze(2).to_broadcast(shape),
                op=MULT,
            )

        def add_tile(result, per, m):
            width = per * TOKEN_TILES * HEAD_DIM
            first = result[:, 0:width].rearrange("p (h m s r) -> p h m s r", h=per, m=TOKEN_TILES, s=2)
            second = result[:, width : TERMS * width].rearrange("p (h m s r) -> p h m s r", h=per, m=TOKEN_TILES, s=2)
            for here in range(2):
                nc.vector.tensor_tensor(
                    out=first[:, :, m, here, :], in0=first[:, :, m, here, :], in1=second[:, :, m, 1 - here, :], op=ADD
                )

        def store(result, row, per):
            width = per * TOKEN_TILES * HEAD_DIM
            head = (row % WIDTH) // HEAD_DIM
            for b in range(BATCH):
                nc.sync.dma_start(
                    out=outs[row // WIDTH][b, head : head + per, :, :].rearrange("h (s m) d -> s h (m d)", m=TOKEN_TILES),
                    in_=result[b:P:BATCH, 0:width].rearrange("p (h f) -> p h f", h=per),
                )

        x_raws = [load_tokens(m) for m in range(TOKEN_TILES)]
        load_next_round()
        load_next_round()
        cos_bf16 = load_table(cos, "cos_bf16")
        sin_bf16 = load_table(sin, "sin_bf16")
        while len(w_raws) < RAW_BUFS:
            load_next_round()

        ident = const.tile([P, P], F32)
        make_identity(nc, ident[:])

        zeros = const.tile([P, BANK_WORDS], BF16)
        nc.vector.memset(zeros[:], 0.0)
        unread = acc_psum.tile([P, MAX_ROWS * P], F32, name="acc", tag="acc")

        def idle_matmuls(count):
            for turn in range(count):
                nc.tensor.matmul(out=unread[:], lhsT=zeros[:, 0:P], rhs=zeros[:], start=True, stop=True)

        idle_matmuls(WARM_UP)

        x_mx = [new_operand(const, "x%d" % m, 1) for m in range(TOKEN_TILES)]
        for m in range(TOKEN_TILES):
            fill_operand(x_mx[m], x_raws[m], 1, range(chunk_count(1)), True)
            idle_matmuls(KEEP_WARM[m])

        tables = const.tile([P, TOKEN_TILES, TERMS, HEAD_DIM], F32)

        def make_tables():
            nc.vector.tensor_copy(out=tables[:, :, 0, :], in_=cos_bf16[:])
            nc.vector.tensor_copy(out=tables[:, :, 1, 0:HALF], in_=sin_bf16[:, :, HALF:HEAD_DIM])
            nc.vector.tensor_scalar_mul(out=tables[:, :, 1, HALF:HEAD_DIM], in0=sin_bf16[:, :, 0:HALF], scalar1=-1.0)

        units = []
        for i, (row, per) in enumerate(rounds):
            for part in range(per // UNIT_ROWS):
                units.append((i, part, per // UNIT_ROWS))
        passes = [(m, g) for m in range(TOKEN_TILES) for g in range(PASSES)]
        operands = {}
        results = {}
        accs = {}

        def part_of(count, part, parts):
            return range(count * part // parts, count * (part + 1) // parts)

        waiting = []

        def is_rotated(i):
            return rounds[i][0] < V * WIDTH

        def put_off(i):
            plain = [j for j in range(i + 1, len(rounds)) if not is_rotated(j)]
            return is_rotated(i) and rounds[i][1] == MAX_ROWS and any(is_rotated(j) for j in range(plain[0], len(rounds)))

        def flip_unit(u):
            i, part, parts = units[u]
            per = rounds[i][1]
            if part == 0:
                operands[i] = new_operand(mx_pool, "w", per)
            fill_operand(operands[i], w_raws[i], per, part_of(chunk_count(per), part, parts), u < HELPED_UNITS)
            if part == parts - 1:
                load_next_round()

        def multiply_unit(u, piece, pieces):
            i, part, parts = units[u]
            row, per = rounds[i]
            rotated = row < V * WIDTH
            part, parts = part * pieces + piece, parts * pieces
            if part == 0:
                if rotated:
                    results[i] = rotated_pool.tile([P, TERMS * per * TOKEN_TILES * HEAD_DIM], F32, name="both", tag="both")
                else:
                    results[i] = plain_pool.tile([P, per * TOKEN_TILES * HEAD_DIM], F32, name="plain", tag="plain")
            for index in part_of(len(passes), part, parts):
                m, g = passes[index]
                if g == 0:
                    accs[0] = acc_psum.tile([P, MAX_ROWS * P], F32, name="acc", tag="acc")
                one_pass(accs[0], operands[i], per, m, g)
                if g == PASSES - 1:
                    empty_psum(accs[0], m, per, results[i], rotated)
                    if rotated and m > 0 and not put_off(i):
                        add_tile(results[i], per, m - 1)
            if not rotated and waiting:
                late = waiting.pop(0)
                for m in range(TOKEN_TILES):
                    add_tile(results[late], rounds[late][1], m)
                store(results[late], rounds[late][0], rounds[late][1])
            if part == parts - 1:
                if rotated and put_off(i):
                    waiting.append(i)
                else:
                    if rotated:
                        add_tile(results[i], per, TOKEN_TILES - 1)
                    store(results[i], row, per)

        flipped = 0
        for u in range(len(units)):
            lead = LEAD_EARLY if u < EARLY_UNITS else LEAD
            due = min(len(units), u + lead) - flipped
            pieces = due if u > 0 and due > 1 else 1
            for piece in range(pieces):
                while flipped < min(len(units), u + lead) - (pieces - 1 - piece):
                    flip_unit(flipped)
                    if flipped == 0:
                        idle_matmuls(KEEP_WARM[TOKEN_TILES])
                    flipped += 1
                if u == 0:
                    make_tables()
                multiply_unit(u, piece, pieces)
